import numpy as np
import ml_dtypes


def mxq(x, axis, fmt="e4m3"):
    dtype, down = {"e4m3": (ml_dtypes.float8_e4m3fn, 7), "e5m2": (ml_dtypes.float8_e5m2, 14)}[fmt]
    v = np.moveaxis(np.asarray(x, np.float32).astype(ml_dtypes.bfloat16).astype(np.float64), axis, -1)
    blocks = v.reshape(v.shape[:-1] + (-1, 32))
    amax = np.abs(blocks).max(-1, keepdims=True)
    byte = np.maximum(np.where(amax > 0, np.frexp(amax)[1] - 1 + 127, 0) - down, 1)
    scale = np.exp2(byte - 127.0)
    codes = (blocks / scale).astype(np.float32).astype(dtype).astype(np.float64)
    return np.moveaxis((codes * scale).reshape(v.shape), -1, axis)


WIDE = False


def mx_kscale(k):
    if not WIDE:
        return np.ones(k)
    levels = np.array([10, -10, 5, -5, 0])
    if k % 512:
        return np.exp2(np.random.permutation(np.resize(levels, k // 32))).repeat(32)
    a = np.empty((k // 512, 16))
    for p in range(k // 512):
        a[p, :8] = np.random.permutation(np.resize(levels, 8))
        for g in range(8):
            far = levels[np.abs(levels - a[p, g]) >= 10]
            a[p, g + 8] = far[np.random.randint(len(far))]
    return np.exp2(a.ravel()).repeat(32)


BF16 = ml_dtypes.bfloat16


def bf(x):
    return np.asarray(x, np.float32).astype(BF16)


def f64(x):
    return np.asarray(x).astype(np.float64)


E2M1 = np.array([0.0, 0.5, 1.0, 1.5, 2.0, 3.0, 4.0, 6.0, -0.0, -0.5, -1.0, -1.5, -2.0, -3.0, -4.0, -6.0])


def pack_weight(w, fmt):
    k, n = w.shape
    w = f64(bf(w)).reshape(k // 32, 32, n)
    amax = np.abs(w).max(1)
    if fmt == "e4m3":
        byte = np.frexp(amax)[1] - 1 + 127 - 7
    else:
        mant, ex = np.frexp(amax / 6.0)
        byte = np.where(mant > 0.5, ex, ex - 1) + 127
    byte = np.clip(np.where(amax > 0, byte, 1), 1, 254)
    scaled = (w * np.exp2(127.0 - byte)[:, None, :]).reshape(k, n).astype(np.float32)
    by_word = np.ascontiguousarray(scaled.reshape(k // 512, 128, 4, n).transpose(0, 1, 3, 2))
    if fmt == "e4m3":
        words = by_word.astype(ml_dtypes.float8_e4m3fn).view(np.uint8)
    else:
        c = by_word.astype(ml_dtypes.float4_e2m1fn).view(np.uint8) & 0xF
        words = c[..., 0::2] | (c[..., 1::2] << 4)
    return np.ascontiguousarray(words), np.ascontiguousarray(byte.astype(np.uint8).reshape(k // 512, 16, n))


def unpack_weight(words, scales, fmt):
    g, p, n, _ = words.shape
    if fmt == "e4m3":
        vals = np.ascontiguousarray(words).view(ml_dtypes.float8_e4m3fn).astype(np.float64)
    else:
        nib = np.empty((g, p, n, 4), np.uint8)
        nib[..., 0::2] = words & 0xF
        nib[..., 1::2] = words >> 4
        vals = E2M1[nib]
    vals = vals * np.repeat(np.exp2(scales.astype(np.float64) - 127.0), 8, axis=1)[..., None]
    return vals.transpose(0, 1, 3, 2).reshape(g * 512, n)


B, T, KA, KT, DIM, NH, HD, E = 16, 512, 256, 256, 512, 8, 128, 8
EPS = 1e-5


def draw0():
    r = np.random.standard_normal
    s = mx_kscale(DIM)
    t = mx_kscale(DIM)
    h_attn = bf(r((B, T, DIM)) * 0.4 * s)
    x = bf(r((B, T, DIM)))
    W_o_words, W_o_scales = pack_weight((r((DIM, DIM)) * 2.0 / np.sqrt(DIM) / s[None, :]).T, "e4m3")
    b_o = bf(r(DIM) * 0.3 + 0.2)
    W_ffn_words, W_ffn_scales = pack_weight((r((DIM, DIM)) / np.sqrt(DIM) / t[None, :]).T, "e4m3")
    return {"h_attn": h_attn,
            "x": x,
            "W_o_words": W_o_words,
            "W_o_scales": W_o_scales,
            "b_o": b_o,
            "W_ffn_words": W_ffn_words,
            "W_ffn_scales": W_ffn_scales,
            "b_ffn": bf(r(DIM) * 0.3),
            "gamma": bf((1.0 + 0.1 * r(DIM)) * t),
            "beta": bf(0.2 * r(DIM) * t)}


def core(h_attn, x, W_o_words, W_o_scales, b_o, W_ffn_words, W_ffn_scales, b_ffn, gamma, beta):
    y = (mxq(f64(h_attn), 2, "e4m3") @ unpack_weight(W_o_words, W_o_scales, "e4m3")) + f64(b_o) + f64(x)
    mu = y.mean(-1, keepdims=True)
    var = ((y - mu) ** 2).mean(-1, keepdims=True)
    xn = (y - mu) / np.sqrt(var + EPS) * f64(gamma) + f64(beta)
    return np.maximum((mxq(xn, 2, "e4m3") @ unpack_weight(W_ffn_words, W_ffn_scales, "e4m3")) + f64(b_ffn), 0.0)


def e4m3fn_bytes(y):
    return np.clip(np.asarray(y, np.float64), -448.0, 448.0).astype(np.float32).astype(ml_dtypes.float8_e4m3fn).view(np.uint8)


def e4m3fn_values(b):
    return np.asarray(b, np.uint8).view(ml_dtypes.float8_e4m3fn).astype(np.float64)


def setup_inputs():
    d = draw0()
    x0 = np.asarray(d['h_attn']).astype(np.float64)
    s = (np.max(np.abs(x0), axis=(0, 1), keepdims=True) / 448.0).astype(np.float32)
    out = {}
    for k, v in d.items():
        if k == 'h_attn':
            out['h_attn_bytes'] = e4m3fn_bytes(x0 / s.astype(np.float64))
            out['h_attn_scale'] = s
        else:
            out[k] = v
    return out


def reference(h_attn_bytes, h_attn_scale, x, W_o_words, W_o_scales, b_o, W_ffn_words, W_ffn_scales, b_ffn, gamma, beta):
    return core(e4m3fn_values(h_attn_bytes) * h_attn_scale.astype(np.float64), x, W_o_words, W_o_scales, b_o, W_ffn_words, W_ffn_scales, b_ffn, gamma, beta)

@@ -1,0 +1,302 @@
+from contextlib import ExitStack
+
+import concourse.mybir as mybir
+from concourse.masks import make_identity
+
+F32 = mybir.dt.float32
+BF16 = mybir.dt.bfloat16
+U8 = mybir.dt.uint8
+U32 = mybir.dt.uint32
+I32 = mybir.dt.int32
+FP8 = mybir.dt.float8_e4m3fn
+FP8X4 = mybir.dt.float8_e4m3fn_x4
+ALU = mybir.AluOpType
+ACT = mybir.ActivationFunctionType
+
+P = 128
+BATCH = 16
+TOK = 512
+DIM = 512
+EPS = 1e-5
+PAIRS = 2 * BATCH
+PT = 256
+
+FLOPS = 2 * 2 * BATCH * TOK * DIM * DIM
+BYTES = BATCH * TOK * DIM * (1 + 2 + 4) + 2 * (DIM * DIM + 16 * DIM) + 4 * DIM + 8 * DIM
+
+
+def relu_on_vector(p):
+    return p % 2 == 0 or p >= PAIRS - 2
+
+
+def tile_l1regressionmoeactionhead_pc_t_w8_kernel(
+    tc, h_bytes, h_scale, x, wo_words, wo_scales, b_o, wf_words, wf_scales, b_ffn, gamma, beta, out
+):
+    nc = tc.nc
+    with ExitStack() as ctx:
+        const = ctx.enter_context(tc.tile_pool(name="const", bufs=1))
+        sb = ctx.enter_context(tc.tile_pool(name="sb", bufs=3))
+        ps = ctx.enter_context(tc.psum_pool(name="ps", bufs=2))
+
+        h_sb, x_sb, xb_sb, hw, hT, hg, hq, hs = {}, {}, {}, {}, {}, {}, {}, {}
+        mm1, y, ysum, ysq, rstd, shift, yn, yT = {}, {}, {}, {}, {}, {}, {}, {}
+        xg, xi, xq, xs, mm2, o = {}, {}, {}, {}, {}, {}
+
+        def load(b):
+            h_t = sb.tile([P, 4 * DIM], U8, name="h_t", bufs=4)
+            src = h_bytes[b].rearrange("(p i) k -> p (i k)", i=4)
+            if b == 0:
+                nc.sync.dma_start(out=h_t[:, 0 : 2 * DIM], in_=src[:, 0 : 2 * DIM])
+                nc.sync.dma_start(out=h_t[:, 2 * DIM : 4 * DIM], in_=src[:, 2 * DIM : 4 * DIM])
+            else:
+                nc.sync.dma_start(out=h_t[:], in_=src)
+            h_sb[b] = h_t
+
+        def load_x(b):
+            x_t = sb.tile([P, 4, DIM], BF16, name="x_t", bufs=4)
+            nc.sync.dma_start(out=x_t[:], in_=x[b].rearrange("(p i) k -> p i k", i=4))
+            x_sb[b] = x_t
+
+        load(0)
+        hsc = const.tile([P, 4], F32, name="hsc")
+        nc.sync.dma_start(out=hsc[:], in_=h_scale.rearrange("a b (p t) -> p (a b t)", t=4))
+        wo_raw = const.tile([P, DIM], U32, name="wo_raw", align_bytes=64)
+        wos_raw = const.tile([P, DIM], U8, name="wos_raw", align_bytes=64)
+        wf_c = const.tile([P, DIM], U32, name="wf_c", align_bytes=64)
+        wf_s = const.tile([P, DIM], U8, name="wf_s", align_bytes=64)
+        nc.vector.memset(wos_raw[:].bitcast(I32), 0)
+        nc.vector.memset(wf_s[:].bitcast(I32), 0)
+        nc.sync.dma_start(out=wo_raw[:].bitcast(I32), in_=wo_words[0].rearrange("p n t -> p (n t)").bitcast(I32))
+        for q in range(4):
+            nc.sync.dma_start(
+                out=wos_raw[32 * q : 32 * q + 4, :].bitcast(I32), in_=wo_scales[0, 4 * q : 4 * q + 4, :].bitcast(I32)
+            )
+        load_x(0)
+        bo_raw = const.tile([P, DIM], BF16, name="bo_raw")
+        bf_bc = const.tile([P, DIM], BF16, name="bf_bc")
+        gb_raw = const.tile([P, 2, 4], BF16, name="gb_raw")
+        nc.scalar.dma_start(out=bo_raw[:], in_=b_o.partition_broadcast(P))
+        nc.scalar.dma_start(out=gb_raw[:, 0, :], in_=gamma.rearrange("(p t) -> p t", t=4))
+        gb_raw2 = const.tile([P, 4], BF16, name="gb_raw2")
+        nc.scalar.dma_start(out=gb_raw2[:], in_=beta.rearrange("(p t) -> p t", t=4))
+        nc.scalar.dma_start(out=bf_bc[:], in_=b_ffn.partition_broadcast(P))
+        load(1)
+        load_x(1)
+        nc.sync.dma_start(out=wf_c[:].bitcast(I32), in_=wf_words[0].rearrange("p n t -> p (n t)").bitcast(I32))
+        for q in range(4):
+            nc.sync.dma_start(
+                out=wf_s[32 * q : 32 * q + 4, :].bitcast(I32), in_=wf_scales[0, 4 * q : 4 * q + 4, :].bitcast(I32)
+            )
+        load(2)
+        load_x(2)
+
+        ident = const.tile([P, P], F32, name="ident")
+        make_identity(nc, ident[:])
+
+        wo_c = const.tile([P, DIM], U32, name="wo_c", align_bytes=64)
+        wo_s = const.tile([P, DIM], U8, name="wo_s", align_bytes=64)
+        nc.vector.tensor_copy(
+            out=wo_c[:].bitcast(I32).rearrange("p (t m) -> p m t", t=4),
+            in_=wo_raw[:].bitcast(I32).rearrange("p (m t) -> p m t", t=4),
+        )
+        nc.vector.tensor_copy(
+            out=wo_s[:].rearrange("p (t m) -> p m t", t=4), in_=wos_raw[:].rearrange("p (m t) -> p m t", t=4)
+        )
+        bo_c = const.tile([P, 4, P], BF16, name="bo_c")
+        nc.gpsimd.tensor_copy(out=bo_c[:], in_=bo_raw[:].rearrange("p (m t) -> p t m", t=4))
+        gam = const.tile([P, 4], F32, name="gam")
+        bet = const.tile([P, 4], F32, name="bet")
+        nc.gpsimd.tensor_copy(out=gam[:], in_=gb_raw[:, 0, :])
+        nc.gpsimd.tensor_copy(out=bet[:], in_=gb_raw2[:])
+
+        def residual(p):
+            b, j = divmod(p, 2)
+            t = sb.tile([P, 2, DIM], F32, name="xb_t")
+            for i in range(2):
+                nc.gpsimd.tensor_tensor(
+                    out=t[:, i, :].rearrange("p (t m) -> p t m", t=4),
+                    in0=x_sb[b][:, 2 * j + i, :].rearrange("p (m t) -> p t m", t=4),
+                    in1=bo_c[:],
+                    op=ALU.add,
+                )
+            xb_sb[p] = t
+
+        def widen(p):
+            b, j = divmod(p, 2)
+            t = sb.tile([P, 2, DIM], BF16, name="hw_t", align_bytes=64)
+            nc.scalar.copy(
+                out=t[:].rearrange("p i k -> p (i k)"),
+                in_=h_sb[b][:, 2 * DIM * j : 2 * DIM * (j + 1)].bitcast(FP8),
+            )
+            hw[p] = t
+
+        def turn_h(p):
+            t = ps.tile([P, 2, PT], F32, name="hT_t")
+            for i in range(2):
+                words = hw[p][:, i, :].bitcast(F32)
+                for u in range(2):
+                    nc.tensor.transpose(t[:, u, P * i : P * (i + 1)], words[:, u : DIM // 2 : 2], ident[:])
+            hT[p] = t
+
+        def scale_h(p):
+            t = sb.tile([P, PT, 4], BF16, name="hg_t", align_bytes=64)
+            nc.vector.tensor_tensor(
+                out=t[:].rearrange("p c (u e) -> p c u e", e=2),
+                in0=hT[p][:].bitcast(BF16).rearrange("p u (c e) -> p c u e", e=2),
+                in1=hsc[:].rearrange("p (u e) -> p u e", e=2).unsqueeze(1).to_broadcast([P, PT, 2, 2]),
+                op=ALU.mult,
+            )
+            hg[p] = t
+
+        def quant_h(p):
+            c = sb.tile([P, PT], U32, name="hq_t", align_bytes=64)
+            s = sb.tile([P, PT], U8, name="hs_t", align_bytes=64)
+            nc.vector.quantize_mx(out=c[:].bitcast(FP8X4), scales=s[:], in_=hg[p][:].rearrange("p c t -> p (c t)"))
+            hq[p], hs[p] = c, s
+
+        def matmul_1(p):
+            tiles = []
+            for i in range(2):
+                t = ps.tile([P, DIM], F32, name="mm1_t")
+                cols = slice(P * i, P * (i + 1))
+                nc.tensor.matmul_mx(
+                    out=t[:], lhsT=hq[p][:, cols].bitcast(FP8X4), lhsT_scale=hs[p][:, cols],
+                    rhs=wo_c[:].bitcast(FP8X4), rhs_scale=wo_s[:], start=True, stop=True,
+                )
+                tiles.append(t)
+            mm1[p] = tiles
+
+        def add_residual(p):
+            t = sb.tile([P, 2, DIM], F32, name="y_t")
+            s = sb.tile([P, 2], F32, name="ysum_t")
+            for i in range(2):
+                nc.vector.scalar_tensor_tensor(
+                    out=t[:, i, :], in0=mm1[p][i][:], scalar=1.0, in1=xb_sb[p][:, i, :],
+                    op0=ALU.mult, op1=ALU.add, accum_out=s[:, i : i + 1],
+                )
+            y[p], ysum[p] = t, s
+
+        def square_sums(p):
+            s = sb.tile([P, 2], F32, name="ysq_t")
+            r = sb.tile([P, 2], F32, name="rstd_t")
+            for i in range(2):
+                junk = sb.tile([P, DIM], BF16, name="junk_t", bufs=2)
+                nc.scalar.activation(
+                    out=junk[:], in_=y[p][:, i, :], func=ACT.Square, scale=-float(DIM),
+                    bias=ysum[p][:, i : i + 1], accum_out=s[:, i : i + 1],
+                )
+            nc.scalar.activation(out=r[:], in_=s[:], func=ACT.Abs_reciprocal_sqrt, scale=float(DIM) ** -3, bias=eps_t[:])
+            ysq[p], rstd[p] = s, r
+
+        def shifts(p):
+            t = sb.tile([P, 2], F32, name="shift_t")
+            nc.vector.scalar_tensor_tensor(
+                out=t[:], in0=ysum[p][:], scalar=-1.0 / DIM, in1=rstd[p][:], op0=ALU.mult, op1=ALU.mult
+            )
+            shift[p] = t
+
+        def normalize(p):
+            t = sb.tile([P, 2, DIM], F32, name="yn_t", align_bytes=64)
+            for i in range(2):
+                nc.scalar.activation(
+                    out=t[:, i, :], in_=y[p][:, i, :], func=ACT.Identity,
+                    scale=rstd[p][:, i : i + 1], bias=shift[p][:, i : i + 1],
+                )
+            yn[p] = t
+
+        def turn_y(p):
+            low = ps.tile([P, 2, PT], F32, name="yT_t")
+            high = ps.tile([P, 2, PT], F32, name="yT_t")
+            banks = [low, high]
+            for i in range(2):
+                for t in range(4):
+                    nc.tensor.transpose(
+                        banks[t // 2][:, t % 2, P * i : P * (i + 1)], yn[p][:, i, P * t : P * (t + 1)], ident[:]
+                    )
+            yT[p] = banks
+
+        def affine(p):
+            g = sb.tile([P, 4, PT], BF16, name="xg_t", align_bytes=64)
+            for t in range(4):
+                nc.scalar.activation(
+                    out=g[:, t, :], in_=yT[p][t // 2][:, t % 2, :], func=ACT.Identity,
+                    scale=gam[:, t : t + 1], bias=bet[:, t : t + 1],
+                )
+            xg[p] = g
+
+        def interleave(p):
+            t = sb.tile([P, PT, 4], BF16, name="xi_t", align_bytes=64)
+            nc.vector.tensor_copy(out=t[:], in_=xg[p][:].rearrange("p t c -> p c t"))
+            xi[p] = t
+
+        def quant_x(p):
+            c = sb.tile([P, PT], U32, name="xq_t", align_bytes=64)
+            s = sb.tile([P, PT], U8, name="xs_t", align_bytes=64)
+            nc.vector.quantize_mx(out=c[:].bitcast(FP8X4), scales=s[:], in_=xi[p][:].rearrange("p c t -> p (c t)"))
+            xq[p], xs[p] = c, s
+
+        def matmul_2(p):
+            tiles = []
+            for i in range(2):
+                t = ps.tile([P, DIM], F32, name="mm2_t")
+                cols = slice(P * i, P * (i + 1))
+                nc.tensor.matmul_mx(
+                    out=t[:], lhsT=xq[p][:, cols].bitcast(FP8X4), lhsT_scale=xs[p][:, cols],
+                    rhs=wf_c[:].bitcast(FP8X4), rhs_scale=wf_s[:], start=True, stop=True,
+                )
+                tiles.append(t)
+            mm2[p] = tiles
+
+        def add_bias(p):
+            t = sb.tile([P, 2, DIM], F32, name="o_t", bufs=4)
+            for i in range(2):
+                nc.vector.tensor_tensor(out=t[:, i, :], in0=mm2[p][i][:], in1=bf_bc[:], op=ALU.add)
+            o[p] = t
+
+        def relu_store(p):
+            b, j = divmod(p, 2)
+            t = o[p]
+            if relu_on_vector(p):
+                nc.vector.tensor_scalar(out=t[:], in0=t[:], scalar1=0.0, scalar2=None, op0=ALU.max)
+            else:
+                nc.scalar.activation(out=t[:], in_=t[:], func=ACT.Relu)
+            nc.sync.dma_start(
+                out=out[b].rearrange("(p i) n -> p i n", i=4)[:, 2 * j : 2 * j + 2, :], in_=t[:]
+            )
+
+        eps_t = const.tile([P, 1], F32, name="eps_t")
+        nc.vector.memset(eps_t[:], EPS)
+        warm = const.tile([P, 1], F32, name="warm")
+        nc.scalar.activation(out=warm[:], in_=eps_t[:], func=ACT.Abs_reciprocal_sqrt)
+
+        def run(stage, p):
+            if 0 <= p < PAIRS:
+                stage(p)
+
+        residual(0)
+        residual(1)
+        for s in range(-2, PAIRS + 4):
+            if s >= 2 and s % 2 == 0 and s // 2 + 2 < BATCH:
+                load(s // 2 + 2)
+                load_x(s // 2 + 2)
+            if s >= 0:
+                run(residual, s + 2)
+            run(add_residual, s)
+            if relu_on_vector(s - 3):
+                run(relu_store, s - 3)
+            run(square_sums, s)
+            run(interleave, s - 1)
+            run(scale_h, s + 1)
+            run(shifts, s)
+            run(widen, s + 2)
+            run(turn_h, s + 2)
+            run(quant_x, s - 1)
+            run(quant_h, s + 1)
+            run(matmul_1, s + 1)
+            run(normalize, s)
+            run(turn_y, s)
+            run(add_bias, s - 2)
+            run(matmul_2, s - 1)
+            if not relu_on_vector(s - 3):
+                run(relu_store, s - 3)
+            run(affine, s)

@@ -26,7 +26,7 @@ BYTES = BATCH * TOK * DIM * (1 + 2 + 4) + 2 * (DIM * DIM + 16 * DIM) + 4 * DIM +
 
 
 def relu_on_vector(p):
-    return p % 2 == 0 or p >= PAIRS - 2
+    return p % 4 == 0 or p >= PAIRS - 2
 
 
 def tile_l1regressionmoeactionhead_pc_t_w8_kernel(
@@ -35,15 +35,16 @@ def tile_l1regressionmoeactionhead_pc_t_w8_kernel(
     nc = tc.nc
     with ExitStack() as ctx:
         const = ctx.enter_context(tc.tile_pool(name="const", bufs=1))
-        sb = ctx.enter_context(tc.tile_pool(name="sb", bufs=3))
+        sb = ctx.enter_context(tc.tile_pool(name="sb", bufs=4))
         ps = ctx.enter_context(tc.psum_pool(name="ps", bufs=2))
+        ctx.enter_context(tc.manual_schedule())
 
         h_sb, x_sb, xb_sb, hw, hT, hg, hq, hs = {}, {}, {}, {}, {}, {}, {}, {}
         mm1, y, ysum, ysq, rstd, shift, yn, yT = {}, {}, {}, {}, {}, {}, {}, {}
         xg, xi, xq, xs, mm2, o = {}, {}, {}, {}, {}, {}
 
         def load(b):
-            h_t = sb.tile([P, 4 * DIM], U8, name="h_t", bufs=4)
+            h_t = sb.tile([P, 4 * DIM], U8, name="h_t", bufs=6)
             src = h_bytes[b].rearrange("(p i) k -> p (i k)", i=4)
             if b == 0:
                 nc.sync.dma_start(out=h_t[:, 0 : 2 * DIM], in_=src[:, 0 : 2 * DIM])
@@ -53,11 +54,15 @@ def tile_l1regressionmoeactionhead_pc_t_w8_kernel(
             h_sb[b] = h_t
 
         def load_x(b):
-            x_t = sb.tile([P, 4, DIM], BF16, name="x_t", bufs=4)
+            x_t = sb.tile([P, 4, DIM], BF16, name="x_t", bufs=6)
             nc.sync.dma_start(out=x_t[:], in_=x[b].rearrange("(p i) k -> p i k", i=4))
             x_sb[b] = x_t
 
         load(0)
+        eps_t = const.tile([P, 1], F32, name="eps_t")
+        nc.vector.memset(eps_t[:], EPS)
+        warm = const.tile([P, 1], F32, name="warm")
+        nc.scalar.activation(out=warm[:], in_=eps_t[:], func=ACT.Abs_reciprocal_sqrt)
         hsc = const.tile([P, 4], F32, name="hsc")
         nc.sync.dma_start(out=hsc[:], in_=h_scale.rearrange("a b (p t) -> p (a b t)", t=4))
         wo_raw = const.tile([P, DIM], U32, name="wo_raw", align_bytes=64)
@@ -109,17 +114,17 @@ def tile_l1regressionmoeactionhead_pc_t_w8_kernel(
         nc.gpsimd.tensor_copy(out=gam[:], in_=gb_raw[:, 0, :])
         nc.gpsimd.tensor_copy(out=bet[:], in_=gb_raw2[:])
 
-        def residual(p):
+        def residual(p, i):
             b, j = divmod(p, 2)
-            t = sb.tile([P, 2, DIM], F32, name="xb_t")
-            for i in range(2):
+            t = sb.tile([P, DIM], F32, name="xb_t", bufs=8)
+            for r in range(0, 4, 2):
                 nc.gpsimd.tensor_tensor(
-                    out=t[:, i, :].rearrange("p (t m) -> p t m", t=4),
-                    in0=x_sb[b][:, 2 * j + i, :].rearrange("p (m t) -> p t m", t=4),
-                    in1=bo_c[:],
+                    out=t[:, P * r : P * (r + 2)].rearrange("p (t m) -> p t m", t=2),
+                    in0=x_sb[b][:, 2 * j + i, :].rearrange("p (m t) -> p t m", t=4)[:, r : r + 2, :],
+                    in1=bo_c[:, r : r + 2, :],
                     op=ALU.add,
                 )
-            xb_sb[p] = t
+            xb_sb[p, i] = t
 
         def widen(p):
             b, j = divmod(p, 2)
@@ -166,67 +171,71 @@ def tile_l1regressionmoeactionhead_pc_t_w8_kernel(
                 tiles.append(t)
             mm1[p] = tiles
 
-        def add_residual(p):
-            t = sb.tile([P, 2, DIM], F32, name="y_t")
-            s = sb.tile([P, 2], F32, name="ysum_t")
-            for i in range(2):
-                nc.vector.scalar_tensor_tensor(
-                    out=t[:, i, :], in0=mm1[p][i][:], scalar=1.0, in1=xb_sb[p][:, i, :],
-                    op0=ALU.mult, op1=ALU.add, accum_out=s[:, i : i + 1],
-                )
-            y[p], ysum[p] = t, s
+        def add_residual(p, i):
+            if p not in ysum:
+                ysum[p] = sb.tile([P, 2], F32, name="ysum_t")
+            t = sb.tile([P, DIM], F32, name="y_t", bufs=8)
+            nc.vector.scalar_tensor_tensor(
+                out=t[:], in0=mm1[p][i][:], scalar=1.0, in1=xb_sb[p, i][:],
+                op0=ALU.mult, op1=ALU.add, accum_out=ysum[p][:, i : i + 1],
+            )
+            y[p, i] = t
 
-        def square_sums(p):
-            s = sb.tile([P, 2], F32, name="ysq_t")
+        def square_sum(p, i):
+            if p not in ysq:
+                ysq[p] = sb.tile([P, 2], F32, name="ysq_t")
+            junk = sb.tile([P, DIM], BF16, name="junk_t", bufs=2)
+            nc.scalar.activation(
+                out=junk[:], in_=y[p, i][:], func=ACT.Square, scale=-float(DIM),
+                bias=ysum[p][:, i : i + 1], accum_out=ysq[p][:, i : i + 1],
+            )
+
+        def inverse_std(p):
             r = sb.tile([P, 2], F32, name="rstd_t")
-            for i in range(2):
-                junk = sb.tile([P, DIM], BF16, name="junk_t", bufs=2)
-                nc.scalar.activation(
-                    out=junk[:], in_=y[p][:, i, :], func=ACT.Square, scale=-float(DIM),
-                    bias=ysum[p][:, i : i + 1], accum_out=s[:, i : i + 1],
-                )
-            nc.scalar.activation(out=r[:], in_=s[:], func=ACT.Abs_reciprocal_sqrt, scale=float(DIM) ** -3, bias=eps_t[:])
-            ysq[p], rstd[p] = s, r
+            nc.scalar.activation(out=r[:], in_=ysq[p][:], func=ACT.Abs_reciprocal_sqrt, scale=float(DIM) ** -3, bias=eps_t[:])
+            rstd[p] = r
 
         def shifts(p):
             t = sb.tile([P, 2], F32, name="shift_t")
-            nc.vector.scalar_tensor_tensor(
-                out=t[:], in0=ysum[p][:], scalar=-1.0 / DIM, in1=rstd[p][:], op0=ALU.mult, op1=ALU.mult
-            )
+            for i in range(2):
+                col = slice(i, i + 1)
+                nc.vector.tensor_scalar(
+                    out=t[:, col], in0=ysum[p][:, col], scalar1=-1.0 / DIM, scalar2=rstd[p][:, col],
+                    op0=ALU.mult, op1=ALU.mult,
+                )
             shift[p] = t
 
-        def normalize(p):
-            t = sb.tile([P, 2, DIM], F32, name="yn_t", align_bytes=64)
-            for i in range(2):
-                nc.scalar.activation(
-                    out=t[:, i, :], in_=y[p][:, i, :], func=ACT.Identity,
-                    scale=rstd[p][:, i : i + 1], bias=shift[p][:, i : i + 1],
-                )
-            yn[p] = t
+        def normalize(p, i):
+            t = sb.tile([P, DIM], F32, name="yn_t", align_bytes=64, bufs=8)
+            nc.scalar.activation(
+                out=t[:], in_=y[p, i][:], func=ACT.Identity,
+                scale=rstd[p][:, i : i + 1], bias=shift[p][:, i : i + 1],
+            )
+            yn[p, i] = t
 
-        def turn_y(p):
-            low = ps.tile([P, 2, PT], F32, name="yT_t")
-            high = ps.tile([P, 2, PT], F32, name="yT_t")
-            banks = [low, high]
-            for i in range(2):
-                for t in range(4):
-                    nc.tensor.transpose(
-                        banks[t // 2][:, t % 2, P * i : P * (i + 1)], yn[p][:, i, P * t : P * (t + 1)], ident[:]
-                    )
-            yT[p] = banks
-
-        def affine(p):
-            g = sb.tile([P, 4, PT], BF16, name="xg_t", align_bytes=64)
+        def turn_y(p, i):
+            if p not in yT:
+                low = ps.tile([P, 2, PT], F32, name="yT_t")
+                high = ps.tile([P, 2, PT], F32, name="yT_t")
+                yT[p] = [low, high]
             for t in range(4):
-                nc.scalar.activation(
-                    out=g[:, t, :], in_=yT[p][t // 2][:, t % 2, :], func=ACT.Identity,
-                    scale=gam[:, t : t + 1], bias=bet[:, t : t + 1],
+                nc.tensor.transpose(
+                    yT[p][t // 2][:, t % 2, P * i : P * (i + 1)], yn[p, i][:, P * t : P * (t + 1)], ident[:]
                 )
-            xg[p] = g
+
+        def affine(p, t):
+            if p not in xg:
+                xg[p] = sb.tile([P, 4, PT], BF16, name="xg_t", align_bytes=64)
+            nc.scalar.activation(
+                out=xg[p][:, t, :], in_=yT[p][t // 2][:, t % 2, :], func=ACT.Identity,
+                scale=gam[:, t : t + 1], bias=bet[:, t : t + 1],
+            )
 
         def interleave(p):
             t = sb.tile([P, PT, 4], BF16, name="xi_t", align_bytes=64)
-            nc.vector.tensor_copy(out=t[:], in_=xg[p][:].rearrange("p t c -> p c t"))
+            nc.vector.tensor_copy(
+                out=t[:].rearrange("p (c i) t -> p c t i", i=4), in_=xg[p][:].rearrange("p t (c i) -> p c t i", i=4)
+            )
             xi[p] = t
 
         def quant_x(p):
@@ -247,56 +256,69 @@ def tile_l1regressionmoeactionhead_pc_t_w8_kernel(
                 tiles.append(t)
             mm2[p] = tiles
 
-        def add_bias(p):
-            t = sb.tile([P, 2, DIM], F32, name="o_t", bufs=4)
-            for i in range(2):
-                nc.vector.tensor_tensor(out=t[:, i, :], in0=mm2[p][i][:], in1=bf_bc[:], op=ALU.add)
-            o[p] = t
+        def add_bias(p, i):
+            if p not in o:
+                o[p] = sb.tile([P, 2, DIM], F32, name="o_t")
+            nc.vector.tensor_tensor(out=o[p][:, i, :], in0=mm2[p][i][:], in1=bf_bc[:], op=ALU.add)
 
-        def relu_store(p):
+        def store(p):
             b, j = divmod(p, 2)
-            t = o[p]
-            if relu_on_vector(p):
-                nc.vector.tensor_scalar(out=t[:], in0=t[:], scalar1=0.0, scalar2=None, op0=ALU.max)
-            else:
-                nc.scalar.activation(out=t[:], in_=t[:], func=ACT.Relu)
             nc.sync.dma_start(
-                out=out[b].rearrange("(p i) n -> p i n", i=4)[:, 2 * j : 2 * j + 2, :], in_=t[:]
+                out=out[b].rearrange("(p i) n -> p i n", i=4)[:, 2 * j : 2 * j + 2, :], in_=o[p][:]
             )
 
-        eps_t = const.tile([P, 1], F32, name="eps_t")
-        nc.vector.memset(eps_t[:], EPS)
-        warm = const.tile([P, 1], F32, name="warm")
-        nc.scalar.activation(out=warm[:], in_=eps_t[:], func=ACT.Abs_reciprocal_sqrt)
+        def relu_v(p):
+            if relu_on_vector(p):
+                nc.vector.tensor_scalar(out=o[p][:], in0=o[p][:], scalar1=0.0, scalar2=None, op0=ALU.max)
+                store(p)
 
-        def run(stage, p):
-            if 0 <= p < PAIRS:
-                stage(p)
+        def relu_s(p, i):
+            if not relu_on_vector(p):
+                nc.scalar.activation(out=o[p][:, i, :], in_=o[p][:, i, :], func=ACT.Relu)
+                left[p] = left.get(p, 2) - 1
+                if left[p] == 0:
+                    store(p)
 
-        residual(0)
-        residual(1)
-        for s in range(-2, PAIRS + 4):
-            if s >= 2 and s % 2 == 0 and s // 2 + 2 < BATCH:
-                load(s // 2 + 2)
-                load_x(s // 2 + 2)
-            if s >= 0:
-                run(residual, s + 2)
-            run(add_residual, s)
-            if relu_on_vector(s - 3):
-                run(relu_store, s - 3)
-            run(square_sums, s)
-            run(interleave, s - 1)
-            run(scale_h, s + 1)
-            run(shifts, s)
-            run(widen, s + 2)
-            run(turn_h, s + 2)
-            run(quant_x, s - 1)
-            run(quant_h, s + 1)
-            run(matmul_1, s + 1)
-            run(normalize, s)
-            run(turn_y, s)
-            run(add_bias, s - 2)
-            run(matmul_2, s - 1)
-            if not relu_on_vector(s - 3):
-                run(relu_store, s - 3)
-            run(affine, s)
+        left = {}
+
+        order = [
+            (residual, 3, 1),
+            (add_bias, -3, 1),
+            (relu_v, -4),
+            (matmul_1, 2),
+            (add_residual, 2, 1),
+            (turn_h, 4),
+            (interleave, -1),
+            (inverse_std, 1),
+            (normalize, 0, 1),
+            (matmul_2, -2),
+            (add_residual, 2, 0),
+            (quant_h, 3),
+            (normalize, 0, 0),
+            (widen, 6),
+            (residual, 3, 0),
+            (add_bias, -2, 0),
+            (turn_y, 0, 1),
+            (relu_s, -5, 1),
+            (quant_x, -1),
+            (relu_s, -3, 0),
+            (turn_y, 0, 0),
+            (square_sum, 2, 1),
+            (affine, 0, 0),
+            (affine, 0, 2),
+            (shifts, 1),
+            (scale_h, 4),
+            (affine, 0, 1),
+            (square_sum, 2, 0),
+            (affine, 0, 3),
+        ]
+        for s in range(-6, PAIRS + 5):
+            if s % 2 == 0:
+                if 3 <= s // 2 + 5 < BATCH:
+                    load(s // 2 + 5)
+                if 3 <= s // 2 + 4 < BATCH:
+                    load_x(s // 2 + 4)
+            for entry in order:
+                p = s + entry[1]
+                if 0 <= p < PAIRS:
+                    entry[0](p, *entry[2:])

@@ -26,7 +26,7 @@ BYTES = BATCH * TOK * DIM * (1 + 2 + 4) + 2 * (DIM * DIM + 16 * DIM) + 4 * DIM +
 
 
 def relu_on_vector(p):
-    return p % 4 == 0 or p >= PAIRS - 2
+    return p % 2 == 0 or p >= PAIRS - 2
 
 
 def tile_l1regressionmoeactionhead_pc_t_w8_kernel(
@@ -116,14 +116,13 @@ def tile_l1regressionmoeactionhead_pc_t_w8_kernel(
 
         def residual(p, i):
             b, j = divmod(p, 2)
-            t = sb.tile([P, DIM], F32, name="xb_t", bufs=8)
-            for r in range(0, 4, 2):
-                nc.gpsimd.tensor_tensor(
-                    out=t[:, P * r : P * (r + 2)].rearrange("p (t m) -> p t m", t=2),
-                    in0=x_sb[b][:, 2 * j + i, :].rearrange("p (m t) -> p t m", t=4)[:, r : r + 2, :],
-                    in1=bo_c[:, r : r + 2, :],
-                    op=ALU.add,
-                )
+            t = sb.tile([P, DIM], F32, name="xb_t", bufs=2)
+            nc.gpsimd.tensor_tensor(
+                out=t[:].rearrange("p (t m) -> p t m", t=4),
+                in0=x_sb[b][:, 2 * j + i, :].rearrange("p (m t) -> p t m", t=4),
+                in1=bo_c[:],
+                op=ALU.add,
+            )
             xb_sb[p, i] = t
 
         def widen(p):
@@ -199,7 +198,7 @@ def tile_l1regressionmoeactionhead_pc_t_w8_kernel(
             t = sb.tile([P, 2], F32, name="shift_t")
             for i in range(2):
                 col = slice(i, i + 1)
-                nc.vector.tensor_scalar(
+                nc.gpsimd.tensor_scalar(
                     out=t[:, col], in0=ysum[p][:, col], scalar1=-1.0 / DIM, scalar2=rstd[p][:, col],
                     op0=ALU.mult, op1=ALU.mult,
                 )
@@ -282,37 +281,37 @@ def tile_l1regressionmoeactionhead_pc_t_w8_kernel(
         left = {}
 
         order = [
-            (residual, 3, 1),
-            (add_bias, -3, 1),
-            (relu_v, -4),
-            (matmul_1, 2),
-            (add_residual, 2, 1),
-            (turn_h, 4),
-            (interleave, -1),
-            (inverse_std, 1),
-            (normalize, 0, 1),
-            (matmul_2, -2),
-            (add_residual, 2, 0),
-            (quant_h, 3),
-            (normalize, 0, 0),
-            (widen, 6),
-            (residual, 3, 0),
-            (add_bias, -2, 0),
-            (turn_y, 0, 1),
-            (relu_s, -5, 1),
-            (quant_x, -1),
+            (widen, 5),
+            (normalize, -1, 0),
+            (turn_h, 2),
+            (normalize, -1, 1),
+            (turn_y, -1, 0),
             (relu_s, -3, 0),
-            (turn_y, 0, 0),
-            (square_sum, 2, 1),
-            (affine, 0, 0),
-            (affine, 0, 2),
-            (shifts, 1),
-            (scale_h, 4),
-            (affine, 0, 1),
-            (square_sum, 2, 0),
-            (affine, 0, 3),
+            (add_residual, 0, 0),
+            (add_residual, 0, 1),
+            (square_sum, 0, 0),
+            (square_sum, 0, 1),
+            (turn_y, -1, 1),
+            (affine, -1, 1),
+            (affine, -1, 0),
+            (residual, 1, 0),
+            (affine, -1, 3),
+            (affine, -1, 2),
+            (residual, 1, 1),
+            (scale_h, 2),
+            (matmul_2, -2),
+            (matmul_1, 1),
+            (add_bias, -2, 0),
+            (add_bias, -2, 1),
+            (inverse_std, 0),
+            (interleave, -1),
+            (relu_s, -5, 1),
+            (shifts, 0),
+            (quant_h, 2),
+            (quant_x, -1),
+            (relu_v, -4),
         ]
-        for s in range(-6, PAIRS + 5):
+        for s in range(-5, PAIRS + 5):
             if s % 2 == 0:
                 if 3 <= s // 2 + 5 < BATCH:
                     load(s // 2 + 5)

@@ -26,7 +26,7 @@ BYTES = BATCH * TOK * DIM * (1 + 2 + 4) + 2 * (DIM * DIM + 16 * DIM) + 4 * DIM +
 
 
 def relu_on_vector(p):
-    return p % 2 == 0 or p >= PAIRS - 2
+    return p >= PAIRS - 2
 
 
 def tile_l1regressionmoeactionhead_pc_t_w8_kernel(
@@ -232,9 +232,7 @@ def tile_l1regressionmoeactionhead_pc_t_w8_kernel(
 
         def interleave(p):
             t = sb.tile([P, PT, 4], BF16, name="xi_t", align_bytes=64)
-            nc.vector.tensor_copy(
-                out=t[:].rearrange("p (c i) t -> p c t i", i=4), in_=xg[p][:].rearrange("p t (c i) -> p c t i", i=4)
-            )
+            nc.vector.tensor_copy(out=t[:], in_=xg[p][:].rearrange("p t c -> p c t"))
             xi[p] = t
 
         def quant_x(p):
@@ -281,37 +279,37 @@ def tile_l1regressionmoeactionhead_pc_t_w8_kernel(
         left = {}
 
         order = [
-            (widen, 5),
-            (normalize, -1, 0),
-            (turn_h, 2),
             (normalize, -1, 1),
-            (turn_y, -1, 0),
-            (relu_s, -3, 0),
             (add_residual, 0, 0),
-            (add_residual, 0, 1),
-            (square_sum, 0, 0),
-            (square_sum, 0, 1),
-            (turn_y, -1, 1),
-            (affine, -1, 1),
-            (affine, -1, 0),
             (residual, 1, 0),
-            (affine, -1, 3),
-            (affine, -1, 2),
-            (residual, 1, 1),
-            (scale_h, 2),
-            (matmul_2, -2),
-            (matmul_1, 1),
-            (add_bias, -2, 0),
-            (add_bias, -2, 1),
-            (inverse_std, 0),
-            (interleave, -1),
-            (relu_s, -5, 1),
-            (shifts, 0),
-            (quant_h, 2),
-            (quant_x, -1),
+            (turn_h, 3),
+            (matmul_2, -3),
+            (quant_h, 1),
+            (add_residual, 0, 1),
+            (normalize, -1, 0),
+            (relu_s, -6, 1),
+            (widen, 7),
+            (square_sum, 0, 0),
+            (relu_s, -6, 0),
+            (turn_y, -1, 1),
             (relu_v, -4),
+            (scale_h, 2),
+            (turn_y, -1, 0),
+            (square_sum, 0, 1),
+            (add_bias, -3, 0),
+            (affine, -1, 0),
+            (matmul_1, 1),
+            (inverse_std, 0),
+            (interleave, -2),
+            (affine, -1, 3),
+            (affine, -1, 1),
+            (residual, 1, 1),
+            (affine, -1, 2),
+            (shifts, 0),
+            (add_bias, -3, 1),
+            (quant_x, -2),
         ]
-        for s in range(-5, PAIRS + 5):
+        for s in range(-7, PAIRS + 6):
             if s % 2 == 0:
                 if 3 <= s // 2 + 5 < BATCH:
                     load(s // 2 + 5)

@@ -18,6 +18,7 @@ BATCH = 16
 TOK = 512
 DIM = 512
 EPS = 1e-5
+F32_MAX = 3.4028234663852886e38
 PAIRS = 2 * BATCH
 PT = 256
 
@@ -26,7 +27,7 @@ BYTES = BATCH * TOK * DIM * (1 + 2 + 4) + 2 * (DIM * DIM + 16 * DIM) + 4 * DIM +
 
 
 def relu_on_vector(p):
-    return p >= PAIRS - 2
+    return p >= PAIRS - 5
 
 
 def tile_l1regressionmoeactionhead_pc_t_w8_kernel(
@@ -48,7 +49,6 @@ def tile_l1regressionmoeactionhead_pc_t_w8_kernel(
             src = h_bytes[b].rearrange("(p i) k -> p (i k)", i=4)
             if b == 0:
                 nc.sync.dma_start(out=h_t[:, 0 : 2 * DIM], in_=src[:, 0 : 2 * DIM])
-                nc.sync.dma_start(out=h_t[:, 2 * DIM : 4 * DIM], in_=src[:, 2 * DIM : 4 * DIM])
             else:
                 nc.sync.dma_start(out=h_t[:], in_=src)
             h_sb[b] = h_t
@@ -59,6 +59,14 @@ def tile_l1regressionmoeactionhead_pc_t_w8_kernel(
             x_sb[b] = x_t
 
         load(0)
+        bo_raw = const.tile([P, DIM], BF16, name="bo_raw")
+        bf_bc = const.tile([P, DIM], BF16, name="bf_bc")
+        gb_raw = const.tile([P, 4], BF16, name="gb_raw")
+        nc.scalar.dma_start(out=bo_raw[:], in_=b_o.partition_broadcast(P))
+        nc.scalar.dma_start(out=gb_raw[:], in_=gamma.rearrange("(p t) -> p t", t=4))
+        gb_raw2 = const.tile([P, 4], BF16, name="gb_raw2")
+        nc.scalar.dma_start(out=gb_raw2[:], in_=beta.rearrange("(p t) -> p t", t=4))
+        nc.scalar.dma_start(out=bf_bc[:], in_=b_ffn.partition_broadcast(P))
         eps_t = const.tile([P, 1], F32, name="eps_t")
         nc.vector.memset(eps_t[:], EPS)
         warm = const.tile([P, 1], F32, name="warm")
@@ -77,14 +85,10 @@ def tile_l1regressionmoeactionhead_pc_t_w8_kernel(
                 out=wos_raw[32 * q : 32 * q + 4, :].bitcast(I32), in_=wo_scales[0, 4 * q : 4 * q + 4, :].bitcast(I32)
             )
         load_x(0)
-        bo_raw = const.tile([P, DIM], BF16, name="bo_raw")
-        bf_bc = const.tile([P, DIM], BF16, name="bf_bc")
-        gb_raw = const.tile([P, 2, 4], BF16, name="gb_raw")
-        nc.scalar.dma_start(out=bo_raw[:], in_=b_o.partition_broadcast(P))
-        nc.scalar.dma_start(out=gb_raw[:, 0, :], in_=gamma.rearrange("(p t) -> p t", t=4))
-        gb_raw2 = const.tile([P, 4], BF16, name="gb_raw2")
-        nc.scalar.dma_start(out=gb_raw2[:], in_=beta.rearrange("(p t) -> p t", t=4))
-        nc.scalar.dma_start(out=bf_bc[:], in_=b_ffn.partition_broadcast(P))
+        nc.sync.dma_start(
+            out=h_sb[0][:, 2 * DIM : 4 * DIM],
+            in_=h_bytes[0].rearrange("(p i) k -> p (i k)", i=4)[:, 2 * DIM : 4 * DIM],
+        )
         load(1)
         load_x(1)
         nc.sync.dma_start(out=wf_c[:].bitcast(I32), in_=wf_words[0].rearrange("p n t -> p (n t)").bitcast(I32))
@@ -108,11 +112,11 @@ def tile_l1regressionmoeactionhead_pc_t_w8_kernel(
             out=wo_s[:].rearrange("p (t m) -> p m t", t=4), in_=wos_raw[:].rearrange("p (m t) -> p m t", t=4)
         )
         bo_c = const.tile([P, 4, P], BF16, name="bo_c")
-        nc.gpsimd.tensor_copy(out=bo_c[:], in_=bo_raw[:].rearrange("p (m t) -> p t m", t=4))
+        nc.vector.tensor_copy(out=bo_c[:], in_=bo_raw[:].rearrange("p (m t) -> p t m", t=4))
         gam = const.tile([P, 4], F32, name="gam")
         bet = const.tile([P, 4], F32, name="bet")
-        nc.gpsimd.tensor_copy(out=gam[:], in_=gb_raw[:, 0, :])
-        nc.gpsimd.tensor_copy(out=bet[:], in_=gb_raw2[:])
+        nc.vector.tensor_copy(out=gam[:], in_=gb_raw[:])
+        nc.vector.tensor_copy(out=bet[:], in_=gb_raw2[:])
 
         def residual(p, i):
             b, j = divmod(p, 2)
@@ -264,52 +268,70 @@ def tile_l1regressionmoeactionhead_pc_t_w8_kernel(
                 out=out[b].rearrange("(p i) n -> p i n", i=4)[:, 2 * j : 2 * j + 2, :], in_=o[p][:]
             )
 
-        def relu_v(p):
+        def relu_v(p, i):
             if relu_on_vector(p):
-                nc.vector.tensor_scalar(out=o[p][:], in0=o[p][:], scalar1=0.0, scalar2=None, op0=ALU.max)
+                nc.vector.tensor_scalar(
+                    out=o[p][:, i, :], in0=o[p][:, i, :], scalar1=0.0, scalar2=None, op0=ALU.max
+                )
+                b, j = divmod(p, 2)
+                nc.sync.dma_start(
+                    out=out[b].rearrange("(p i) n -> p i n", i=4)[:, 2 * j + i, :], in_=o[p][:, i, :]
+                )
+
+        def count(p):
+            left[p] = left.get(p, 2) - 1
+            if left[p] == 0:
                 store(p)
 
         def relu_s(p, i):
-            if not relu_on_vector(p):
+            if not relu_on_vector(p) and p % 4 < 2:
                 nc.scalar.activation(out=o[p][:, i, :], in_=o[p][:, i, :], func=ACT.Relu)
-                left[p] = left.get(p, 2) - 1
-                if left[p] == 0:
-                    store(p)
+                count(p)
+
+        def relu_g(p, i):
+            if not relu_on_vector(p) and p % 4 >= 2:
+                nc.gpsimd.tensor_scalar(
+                    out=o[p][:, i, :], in0=o[p][:, i, :], scalar1=F32_MAX, scalar2=0.0, op0=ALU.min, op1=ALU.max
+                )
+                count(p)
 
         left = {}
 
         order = [
-            (normalize, -1, 1),
-            (add_residual, 0, 0),
-            (residual, 1, 0),
-            (turn_h, 3),
-            (matmul_2, -3),
-            (quant_h, 1),
-            (add_residual, 0, 1),
             (normalize, -1, 0),
-            (relu_s, -6, 1),
-            (widen, 7),
-            (square_sum, 0, 0),
-            (relu_s, -6, 0),
-            (turn_y, -1, 1),
-            (relu_v, -4),
-            (scale_h, 2),
-            (turn_y, -1, 0),
-            (square_sum, 0, 1),
-            (add_bias, -3, 0),
-            (affine, -1, 0),
             (matmul_1, 1),
+            (relu_g, -6, 0),
+            (square_sum, 0, 1),
+            (turn_y, -1, 1),
+            (square_sum, 0, 0),
+            (turn_y, -1, 0),
             (inverse_std, 0),
-            (interleave, -2),
-            (affine, -1, 3),
-            (affine, -1, 1),
+            (scale_h, 2),
+            (residual, 1, 0),
+            (add_bias, -3, 0),
+            (relu_s, -5, 0),
+            (turn_h, 3),
+            (relu_s, -4, 1),
+            (add_residual, 1, 0),
             (residual, 1, 1),
+            (widen, 4),
+            (affine, -1, 0),
             (affine, -1, 2),
-            (shifts, 0),
-            (add_bias, -3, 1),
+            (interleave, -2),
+            (quant_h, 2),
+            (relu_g, -4, 1),
+            (affine, -1, 3),
             (quant_x, -2),
+            (add_bias, -3, 1),
+            (shifts, 0),
+            (normalize, 0, 1),
+            (add_residual, 1, 1),
+            (matmul_2, -2),
+            (affine, -1, 1),
+            (relu_v, -3, 0),
+            (relu_v, -3, 1),
         ]
-        for s in range(-7, PAIRS + 6):
+        for s in range(-4, PAIRS + 6):
             if s % 2 == 0:
                 if 3 <= s // 2 + 5 < BATCH:
                     load(s // 2 + 5)

from contextlib import ExitStack

import concourse.mybir as mybir
from concourse.masks import make_identity

F32 = mybir.dt.float32
BF16 = mybir.dt.bfloat16
U8 = mybir.dt.uint8
U32 = mybir.dt.uint32
I32 = mybir.dt.int32
FP8 = mybir.dt.float8_e4m3fn
FP8X4 = mybir.dt.float8_e4m3fn_x4
ALU = mybir.AluOpType
ACT = mybir.ActivationFunctionType

P = 128
BATCH = 16
TOK = 512
DIM = 512
EPS = 1e-5
F32_MAX = 3.4028234663852886e38
PAIRS = 2 * BATCH
PT = 256

FLOPS = 2 * 2 * BATCH * TOK * DIM * DIM
BYTES = BATCH * TOK * DIM * (1 + 2 + 4) + 2 * (DIM * DIM + 16 * DIM) + 4 * DIM + 8 * DIM


def relu_on_vector(p):
    return p >= PAIRS - 5


def tile_l1regressionmoeactionhead_pc_t_w8_kernel(
    tc, h_bytes, h_scale, x, wo_words, wo_scales, b_o, wf_words, wf_scales, b_ffn, gamma, beta, out
):
    nc = tc.nc
    with ExitStack() as ctx:
        const = ctx.enter_context(tc.tile_pool(name="const", bufs=1))
        sb = ctx.enter_context(tc.tile_pool(name="sb", bufs=4))
        ps = ctx.enter_context(tc.psum_pool(name="ps", bufs=2))
        ctx.enter_context(tc.manual_schedule())

        h_sb, x_sb, xb_sb, hw, hT, hg, hq, hs = {}, {}, {}, {}, {}, {}, {}, {}
        mm1, y, ysum, ysq, rstd, shift, yn, yT = {}, {}, {}, {}, {}, {}, {}, {}
        xg, xi, xq, xs, mm2, o = {}, {}, {}, {}, {}, {}

        def load(b):
            h_t = sb.tile([P, 4 * DIM], U8, name="h_t", bufs=6)
            src = h_bytes[b].rearrange("(p i) k -> p (i k)", i=4)
            if b == 0:
                nc.sync.dma_start(out=h_t[:, 0 : 2 * DIM], in_=src[:, 0 : 2 * DIM])
            else:
                nc.sync.dma_start(out=h_t[:], in_=src)
            h_sb[b] = h_t

        def load_x(b):
            x_t = sb.tile([P, 4, DIM], BF16, name="x_t", bufs=6)
            nc.sync.dma_start(out=x_t[:], in_=x[b].rearrange("(p i) k -> p i k", i=4))
            x_sb[b] = x_t

        load(0)
        bo_raw = const.tile([P, DIM], BF16, name="bo_raw")
        bf_bc = const.tile([P, DIM], BF16, name="bf_bc")
        gb_raw = const.tile([P, 4], BF16, name="gb_raw")
        nc.scalar.dma_start(out=bo_raw[:], in_=b_o.partition_broadcast(P))
        nc.scalar.dma_start(out=gb_raw[:], in_=gamma.rearrange("(p t) -> p t", t=4))
        gb_raw2 = const.tile([P, 4], BF16, name="gb_raw2")
        nc.scalar.dma_start(out=gb_raw2[:], in_=beta.rearrange("(p t) -> p t", t=4))
        nc.scalar.dma_start(out=bf_bc[:], in_=b_ffn.partition_broadcast(P))
        eps_t = const.tile([P, 1], F32, name="eps_t")
        nc.vector.memset(eps_t[:], EPS)
        warm = const.tile([P, 1], F32, name="warm")
        nc.scalar.activation(out=warm[:], in_=eps_t[:], func=ACT.Abs_reciprocal_sqrt)
        hsc = const.tile([P, 4], F32, name="hsc")
        nc.sync.dma_start(out=hsc[:], in_=h_scale.rearrange("a b (p t) -> p (a b t)", t=4))
        wo_raw = const.tile([P, DIM], U32, name="wo_raw", align_bytes=64)
        wos_raw = const.tile([P, DIM], U8, name="wos_raw", align_bytes=64)
        wf_c = const.tile([P, DIM], U32, name="wf_c", align_bytes=64)
        wf_s = const.tile([P, DIM], U8, name="wf_s", align_bytes=64)
        nc.vector.memset(wos_raw[:].bitcast(I32), 0)
        nc.vector.memset(wf_s[:].bitcast(I32), 0)
        nc.sync.dma_start(out=wo_raw[:].bitcast(I32), in_=wo_words[0].rearrange("p n t -> p (n t)").bitcast(I32))
        for q in range(4):
            nc.sync.dma_start(
                out=wos_raw[32 * q : 32 * q + 4, :].bitcast(I32), in_=wo_scales[0, 4 * q : 4 * q + 4, :].bitcast(I32)
            )
        load_x(0)
        nc.sync.dma_start(
            out=h_sb[0][:, 2 * DIM : 4 * DIM],
            in_=h_bytes[0].rearrange("(p i) k -> p (i k)", i=4)[:, 2 * DIM : 4 * DIM],
        )
        load(1)
        load_x(1)
        nc.sync.dma_start(out=wf_c[:].bitcast(I32), in_=wf_words[0].rearrange("p n t -> p (n t)").bitcast(I32))
        for q in range(4):
            nc.sync.dma_start(
                out=wf_s[32 * q : 32 * q + 4, :].bitcast(I32), in_=wf_scales[0, 4 * q : 4 * q + 4, :].bitcast(I32)
            )
        load(2)
        load_x(2)

        ident = const.tile([P, P], F32, name="ident")
        make_identity(nc, ident[:])

        wo_c = const.tile([P, DIM], U32, name="wo_c", align_bytes=64)
        wo_s = const.tile([P, DIM], U8, name="wo_s", align_bytes=64)
        nc.vector.tensor_copy(
            out=wo_c[:].bitcast(I32).rearrange("p (t m) -> p m t", t=4),
            in_=wo_raw[:].bitcast(I32).rearrange("p (m t) -> p m t", t=4),
        )
        nc.vector.tensor_copy(
            out=wo_s[:].rearrange("p (t m) -> p m t", t=4), in_=wos_raw[:].rearrange("p (m t) -> p m t", t=4)
        )
        bo_c = const.tile([P, 4, P], BF16, name="bo_c")
        nc.vector.tensor_copy(out=bo_c[:], in_=bo_raw[:].rearrange("p (m t) -> p t m", t=4))
        gam = const.tile([P, 4], F32, name="gam")
        bet = const.tile([P, 4], F32, name="bet")
        nc.vector.tensor_copy(out=gam[:], in_=gb_raw[:])
        nc.vector.tensor_copy(out=bet[:], in_=gb_raw2[:])

        def residual(p, i):
            b, j = divmod(p, 2)
            t = sb.tile([P, DIM], F32, name="xb_t", bufs=2)
            nc.gpsimd.tensor_tensor(
                out=t[:].rearrange("p (t m) -> p t m", t=4),
                in0=x_sb[b][:, 2 * j + i, :].rearrange("p (m t) -> p t m", t=4),
                in1=bo_c[:],
                op=ALU.add,
            )
            xb_sb[p, i] = t

        def widen(p):
            b, j = divmod(p, 2)
            t = sb.tile([P, 2, DIM], BF16, name="hw_t", align_bytes=64)
            nc.scalar.copy(
                out=t[:].rearrange("p i k -> p (i k)"),
                in_=h_sb[b][:, 2 * DIM * j : 2 * DIM * (j + 1)].bitcast(FP8),
            )
            hw[p] = t

        def turn_h(p):
            t = ps.tile([P, 2, PT], F32, name="hT_t")
            for i in range(2):
                words = hw[p][:, i, :].bitcast(F32)
                for u in range(2):
                    nc.tensor.transpose(t[:, u, P * i : P * (i + 1)], words[:, u : DIM // 2 : 2], ident[:])
            hT[p] = t

        def scale_h(p):
            t = sb.tile([P, PT, 4], BF16, name="hg_t", align_bytes=64)
            nc.vector.tensor_tensor(
                out=t[:].rearrange("p c (u e) -> p c u e", e=2),
                in0=hT[p][:].bitcast(BF16).rearrange("p u (c e) -> p c u e", e=2),
                in1=hsc[:].rearrange("p (u e) -> p u e", e=2).unsqueeze(1).to_broadcast([P, PT, 2, 2]),
                op=ALU.mult,
            )
            hg[p] = t

        def quant_h(p):
            c = sb.tile([P, PT], U32, name="hq_t", align_bytes=64)
            s = sb.tile([P, PT], U8, name="hs_t", align_bytes=64)
            nc.vector.quantize_mx(out=c[:].bitcast(FP8X4), scales=s[:], in_=hg[p][:].rearrange("p c t -> p (c t)"))
            hq[p], hs[p] = c, s

        def matmul_1(p):
            tiles = []
            for i in range(2):
                t = ps.tile([P, DIM], F32, name="mm1_t")
                cols = slice(P * i, P * (i + 1))
                nc.tensor.matmul_mx(
                    out=t[:], lhsT=hq[p][:, cols].bitcast(FP8X4), lhsT_scale=hs[p][:, cols],
                    rhs=wo_c[:].bitcast(FP8X4), rhs_scale=wo_s[:], start=True, stop=True,
                )
                tiles.append(t)
            mm1[p] = tiles

        def add_residual(p, i):
            if p not in ysum:
                ysum[p] = sb.tile([P, 2], F32, name="ysum_t")
            t = sb.tile([P, DIM], F32, name="y_t", bufs=8)
            nc.vector.scalar_tensor_tensor(
                out=t[:], in0=mm1[p][i][:], scalar=1.0, in1=xb_sb[p, i][:],
                op0=ALU.mult, op1=ALU.add, accum_out=ysum[p][:, i : i + 1],
            )
            y[p, i] = t

        def square_sum(p, i):
            if p not in ysq:
                ysq[p] = sb.tile([P, 2], F32, name="ysq_t")
            junk = sb.tile([P, DIM], BF16, name="junk_t", bufs=2)
            nc.scalar.activation(
                out=junk[:], in_=y[p, i][:], func=ACT.Square, scale=-float(DIM),
                bias=ysum[p][:, i : i + 1], accum_out=ysq[p][:, i : i + 1],
            )

        def inverse_std(p):
            r = sb.tile([P, 2], F32, name="rstd_t")
            nc.scalar.activation(out=r[:], in_=ysq[p][:], func=ACT.Abs_reciprocal_sqrt, scale=float(DIM) ** -3, bias=eps_t[:])
            rstd[p] = r

        def shifts(p):
            t = sb.tile([P, 2], F32, name="shift_t")
            for i in range(2):
                col = slice(i, i + 1)
                nc.gpsimd.tensor_scalar(
                    out=t[:, col], in0=ysum[p][:, col], scalar1=-1.0 / DIM, scalar2=rstd[p][:, col],
                    op0=ALU.mult, op1=ALU.mult,
                )
            shift[p] = t

        def normalize(p, i):
            t = sb.tile([P, DIM], F32, name="yn_t", align_bytes=64, bufs=8)
            nc.scalar.activation(
                out=t[:], in_=y[p, i][:], func=ACT.Identity,
                scale=rstd[p][:, i : i + 1], bias=shift[p][:, i : i + 1],
            )
            yn[p, i] = t

        def turn_y(p, i):
            if p not in yT:
                low = ps.tile([P, 2, PT], F32, name="yT_t")
                high = ps.tile([P, 2, PT], F32, name="yT_t")
                yT[p] = [low, high]
            for t in range(4):
                nc.tensor.transpose(
                    yT[p][t // 2][:, t % 2, P * i : P * (i + 1)], yn[p, i][:, P * t : P * (t + 1)], ident[:]
                )

        def affine(p, t):
            if p not in xg:
                xg[p] = sb.tile([P, 4, PT], BF16, name="xg_t", align_bytes=64)
            nc.scalar.activation(
                out=xg[p][:, t, :], in_=yT[p][t // 2][:, t % 2, :], func=ACT.Identity,
                scale=gam[:, t : t + 1], bias=bet[:, t : t + 1],
            )

        def interleave(p):
            t = sb.tile([P, PT, 4], BF16, name="xi_t", align_bytes=64)
            nc.vector.tensor_copy(out=t[:], in_=xg[p][:].rearrange("p t c -> p c t"))
            xi[p] = t

        def quant_x(p):
            c = sb.tile([P, PT], U32, name="xq_t", align_bytes=64)
            s = sb.tile([P, PT], U8, name="xs_t", align_bytes=64)
            nc.vector.quantize_mx(out=c[:].bitcast(FP8X4), scales=s[:], in_=xi[p][:].rearrange("p c t -> p (c t)"))
            xq[p], xs[p] = c, s

        def matmul_2(p):
            tiles = []
            for i in range(2):
                t = ps.tile([P, DIM], F32, name="mm2_t")
                cols = slice(P * i, P * (i + 1))
                nc.tensor.matmul_mx(
                    out=t[:], lhsT=xq[p][:, cols].bitcast(FP8X4), lhsT_scale=xs[p][:, cols],
                    rhs=wf_c[:].bitcast(FP8X4), rhs_scale=wf_s[:], start=True, stop=True,
                )
                tiles.append(t)
            mm2[p] = tiles

        def add_bias(p, i):
            if p not in o:
                o[p] = sb.tile([P, 2, DIM], F32, name="o_t")
            nc.vector.tensor_tensor(out=o[p][:, i, :], in0=mm2[p][i][:], in1=bf_bc[:], op=ALU.add)

        def store(p):
            b, j = divmod(p, 2)
            nc.sync.dma_start(
                out=out[b].rearrange("(p i) n -> p i n", i=4)[:, 2 * j : 2 * j + 2, :], in_=o[p][:]
            )

        def relu_v(p, i):
            if relu_on_vector(p):
                nc.vector.tensor_scalar(
                    out=o[p][:, i, :], in0=o[p][:, i, :], scalar1=0.0, scalar2=None, op0=ALU.max
                )
                b, j = divmod(p, 2)
                nc.sync.dma_start(
                    out=out[b].rearrange("(p i) n -> p i n", i=4)[:, 2 * j + i, :], in_=o[p][:, i, :]
                )

        def count(p):
            left[p] = left.get(p, 2) - 1
            if left[p] == 0:
                store(p)

        def relu_s(p, i):
            if not relu_on_vector(p) and p % 4 < 2:
                nc.scalar.activation(out=o[p][:, i, :], in_=o[p][:, i, :], func=ACT.Relu)
                count(p)

        def relu_g(p, i):
            if not relu_on_vector(p) and p % 4 >= 2:
                nc.gpsimd.tensor_scalar(
                    out=o[p][:, i, :], in0=o[p][:, i, :], scalar1=F32_MAX, scalar2=0.0, op0=ALU.min, op1=ALU.max
                )
                count(p)

        left = {}

        order = [
            (normalize, -1, 0),
            (matmul_1, 1),
            (relu_g, -6, 0),
            (square_sum, 0, 1),
            (turn_y, -1, 1),
            (square_sum, 0, 0),
            (turn_y, -1, 0),
            (inverse_std, 0),
            (scale_h, 2),
            (residual, 1, 0),
            (add_bias, -3, 0),
            (relu_s, -5, 0),
            (turn_h, 3),
            (relu_s, -4, 1),
            (add_residual, 1, 0),
            (residual, 1, 1),
            (widen, 4),
            (affine, -1, 0),
            (affine, -1, 2),
            (interleave, -2),
            (quant_h, 2),
            (relu_g, -4, 1),
            (affine, -1, 3),
            (quant_x, -2),
            (add_bias, -3, 1),
            (shifts, 0),
            (normalize, 0, 1),
            (add_residual, 1, 1),
            (matmul_2, -2),
            (affine, -1, 1),
            (relu_v, -3, 0),
            (relu_v, -3, 1),
        ]
        for s in range(-4, PAIRS + 6):
            if s % 2 == 0:
                if 3 <= s // 2 + 5 < BATCH:
                    load(s // 2 + 5)
                if 3 <= s // 2 + 4 < BATCH:
                    load_x(s // 2 + 4)
            for entry in order:
                p = s + entry[1]
                if 0 <= p < PAIRS:
                    entry[0](p, *entry[2:])
